import numpy as np
import ml_dtypes


def mxq(x, axis, fmt="e4m3"):
    dtype, down = {"e4m3": (ml_dtypes.float8_e4m3fn, 7), "e5m2": (ml_dtypes.float8_e5m2, 14)}[fmt]
    v = np.moveaxis(np.asarray(x, np.float32).astype(ml_dtypes.bfloat16).astype(np.float64), axis, -1)
    blocks = v.reshape(v.shape[:-1] + (-1, 32))
    amax = np.abs(blocks).max(-1, keepdims=True)
    byte = np.maximum(np.where(amax > 0, np.frexp(amax)[1] - 1 + 127, 0) - down, 1)
    scale = np.exp2(byte - 127.0)
    codes = (blocks / scale).astype(np.float32).astype(dtype).astype(np.float64)
    return np.moveaxis((codes * scale).reshape(v.shape), -1, axis)


WIDE = False


def mx_kscale(k):
    if not WIDE:
        return np.ones(k)
    levels = np.array([10, -10, 5, -5, 0])
    a = np.random.permutation(np.resize(levels, k // 512 * 4)).reshape(k // 512, 4)
    idx = np.arange(k)
    return np.exp2(a[idx // 512, idx % 128 // 32])


BF16 = ml_dtypes.bfloat16


def bf(x):
    return np.asarray(x, np.float32).astype(BF16)


def f64(x):
    return np.asarray(x).astype(np.float64)


E2M1 = np.array([0.0, 0.5, 1.0, 1.5, 2.0, 3.0, 4.0, 6.0, -0.0, -0.5, -1.0, -1.5, -2.0, -3.0, -4.0, -6.0])


def pack_weight(w, fmt):
    k, n = w.shape
    w = f64(bf(w)).reshape(k // 32, 32, n)
    amax = np.abs(w).max(1)
    if fmt == "e4m3":
        byte = np.frexp(amax)[1] - 1 + 127 - 7
    else:
        mant, ex = np.frexp(amax / 6.0)
        byte = np.where(mant > 0.5, ex, ex - 1) + 127
    byte = np.clip(np.where(amax > 0, byte, 1), 1, 254)
    scaled = (w * np.exp2(127.0 - byte)[:, None, :]).reshape(k, n).astype(np.float32)
    by_word = np.ascontiguousarray(scaled.reshape(k // 512, 128, 4, n).transpose(0, 1, 3, 2))
    if fmt == "e4m3":
        words = by_word.astype(ml_dtypes.float8_e4m3fn).view(np.uint8)
    else:
        c = by_word.astype(ml_dtypes.float4_e2m1fn).view(np.uint8) & 0xF
        words = c[..., 0::2] | (c[..., 1::2] << 4)
    return np.ascontiguousarray(words), np.ascontiguousarray(byte.astype(np.uint8).reshape(k // 512, 16, n))


def unpack_weight(words, scales, fmt):
    g, p, n, _ = words.shape
    if fmt == "e4m3":
        vals = np.ascontiguousarray(words).view(ml_dtypes.float8_e4m3fn).astype(np.float64)
    else:
        nib = np.empty((g, p, n, 4), np.uint8)
        nib[..., 0::2] = words & 0xF
        nib[..., 1::2] = words >> 4
        vals = E2M1[nib]
    vals = vals * np.repeat(np.exp2(scales.astype(np.float64) - 127.0), 8, axis=1)[..., None]
    return vals.transpose(0, 1, 3, 2).reshape(g * 512, n)


B, H, W, C, D, P = 128, 1, 1, 512, 16384, 256
F = H * W * D
STRIDE = 16.0
FMT = "e4m3"


def safe_exp(v):
    return np.exp(np.clip(v, -10.0, 10.0))


def setup_inputs():
    s = mx_kscale(C)
    t = mx_kscale(F)[:D]
    tf = np.tile(t, H * W)[:, None]
    features = bf(np.random.standard_normal((B, H, W, C)) * s)
    roi = bf(np.random.uniform(0.02, 0.125, (B, P, 4)))
    conv_w_words, conv_w_scales = pack_weight(np.random.standard_normal((C, D)) / np.sqrt(C) / s[:, None] * t, FMT)
    conv_b = bf(np.random.standard_normal(D) * 0.2 * t)
    cls_w_words, cls_w_scales = pack_weight(np.random.standard_normal((F, 2 * P)) * 1.5 / np.sqrt(F) / tf, FMT)
    cls_b = bf(np.random.standard_normal(2 * P) * 0.5)
    bbox_w_words, bbox_w_scales = pack_weight(np.random.standard_normal((F, 4 * P)) * 0.7 / np.sqrt(F) / tf, FMT)
    bbox_b = bf(np.random.standard_normal(4 * P) * 0.3)
    return {"features": features,
            "roi": roi,
            "conv_w_words": conv_w_words,
            "conv_w_scales": conv_w_scales,
            "conv_b": conv_b,
            "cls_w_words": cls_w_words,
            "cls_w_scales": cls_w_scales,
            "cls_b": cls_b,
            "bbox_w_words": bbox_w_words,
            "bbox_w_scales": bbox_w_scales,
            "bbox_b": bbox_b}


def reference(features, roi, conv_w_words, conv_w_scales, conv_b, cls_w_words, cls_w_scales, cls_b, bbox_w_words, bbox_w_scales, bbox_b):
    h = np.maximum((mxq(f64(features).reshape(B * H * W, C), 1, "e4m3") @ unpack_weight(conv_w_words, conv_w_scales, FMT)) + f64(conv_b), 0.0)
    flatq = mxq(h.reshape(B, F), 1, "e4m3")
    cls = (flatq @ unpack_weight(cls_w_words, cls_w_scales, FMT)) + f64(cls_b)
    bbox = (flatq @ unpack_weight(bbox_w_words, bbox_w_scales, FMT)[:, P:]) + f64(bbox_b)[P:]
    obj = np.stack([cls[:, :P], cls[:, P:]], axis=0)
    e = np.exp(obj - obj.max(axis=0, keepdims=True))
    objectness = (e / e.sum(axis=0, keepdims=True))[1]
    roi_img = f64(roi) * STRIDE
    bb = np.transpose(bbox.reshape(B, 3, P), (0, 2, 1))
    x = roi_img[:, :, 0] - bb[:, :, 0] * roi_img[:, :, 3]
    y = roi_img[:, :, 1]
    w = roi_img[:, :, 2] * safe_exp(bb[:, :, 1])
    hh = roi_img[:, :, 3] * safe_exp(bb[:, :, 2])
    return np.stack([x, y, w, hh, objectness], axis=-1)

@@ -1,0 +1,287 @@
+from contextlib import ExitStack
+
+import concourse.mybir as mybir
+from concourse.masks import make_identity
+
+F32 = mybir.dt.float32
+BF16 = mybir.dt.bfloat16
+I32 = mybir.dt.int32
+U32 = mybir.dt.uint32
+U8 = mybir.dt.uint8
+FP8X4 = mybir.dt.float8_e4m3fn_x4
+ALU = mybir.AluOpType
+ACT = mybir.ActivationFunctionType
+
+P = 128
+PACK = 4
+K_PASS = P * PACK
+BATCH = 128
+CHANNELS = 512
+HIDDEN = 16384
+PROPOSALS = 256
+CLS_COLS = 2 * PROPOSALS
+BOX_SKIP = PROPOSALS
+BOX_COLS = 3 * PROPOSALS
+GROUPS = HIDDEN // K_PASS
+CHUNK = 4
+CHUNKS = GROUPS // CHUNK
+QUADS = 4
+STRIDE = 16.0
+CLIP = 10.0
+
+FLOPS = 2 * BATCH * CHANNELS * HIDDEN + 2 * BATCH * HIDDEN * (CLS_COLS + BOX_COLS)
+BYTES = (
+    (CHANNELS * HIDDEN + HIDDEN * (CLS_COLS + BOX_COLS)) * 33 // 32
+    + 2 * (BATCH * CHANNELS + BATCH * PROPOSALS * 4 + HIDDEN + CLS_COLS + BOX_COLS)
+    + 4 * BATCH * PROPOSALS * 5
+)
+
+
+def tile_classifiermodel_k_kernel(
+    tc,
+    features,
+    roi,
+    conv_w_words,
+    conv_w_scales,
+    conv_b,
+    cls_w_words,
+    cls_w_scales,
+    cls_b,
+    bbox_w_words,
+    bbox_w_scales,
+    bbox_b,
+    out,
+):
+    nc = tc.nc
+    with ExitStack() as stack:
+        keep = stack.enter_context(tc.tile_pool(name="keep", bufs=1))
+        conv_pool = stack.enter_context(tc.tile_pool(name="conv", bufs=3))
+        head_pool = stack.enter_context(tc.tile_pool(name="heads", bufs=4))
+        work = stack.enter_context(tc.tile_pool(name="work", bufs=2))
+        acc_pool = stack.enter_context(tc.psum_pool(name="acc", bufs=1))
+        turn_pool = stack.enter_context(tc.psum_pool(name="turn", bufs=CHUNK))
+        sums_pool = stack.enter_context(tc.psum_pool(name="sums", bufs=1))
+
+        feat_sb = keep.tile([BATCH, CHANNELS], BF16)
+        nc.scalar.dma_start(out=feat_sb[:], in_=features.rearrange("b h w c -> b (h w c)"))
+        conv_b_rows = keep.tile([P, K_PASS], BF16)
+        nc.vector.memset(conv_b_rows[:], 0.0)
+        nc.scalar.dma_start(out=conv_b_rows[0:GROUPS, :], in_=conv_b.rearrange("(g k) -> g k", k=K_PASS))
+
+        conv_planes = keep.tile([P, HIDDEN // CHUNK], U8, align_bytes=64)
+        cls_planes = keep.tile([P, CHUNKS, CLS_COLS], U8, align_bytes=64)
+        box_planes = keep.tile([P, CHUNKS, BOX_COLS], U8, align_bytes=64)
+        nc.vector.memset(conv_planes[:].bitcast(I32), 0)
+        nc.vector.memset(cls_planes[:].bitcast(I32), 0)
+        nc.vector.memset(box_planes[:].bitcast(I32), 0)
+        for quad in range(QUADS):
+            nc.sync.dma_start(
+                out=conv_planes[32 * quad : 32 * quad + 16, :].bitcast(I32),
+                in_=conv_w_scales[0, 4 * quad : 4 * quad + 4, :].rearrange("r (i n) -> i r n", i=CHUNK).bitcast(I32),
+            )
+        for quad in range(QUADS):
+            for r in range(4):
+                rows = slice(32 * quad + r, 32 * quad + 16, 4)
+                nc.sync.dma_start(
+                    out=cls_planes[rows, :, :].bitcast(I32),
+                    in_=cls_w_scales[:, 4 * quad + r, :].rearrange("(c i) n -> i c n", i=CHUNK).bitcast(I32),
+                )
+        for quad in range(QUADS):
+            for r in range(4):
+                rows = slice(32 * quad + r, 32 * quad + 16, 4)
+                nc.sync.dma_start(
+                    out=box_planes[rows, :, :].bitcast(I32),
+                    in_=bbox_w_scales[:, 4 * quad + r, BOX_SKIP:].rearrange("(c i) n -> i c n", i=CHUNK).bitcast(I32),
+                )
+
+        conv_words = {}
+        cls_words = {}
+        box_words = {}
+
+        def load_conv(c):
+            conv_words[c] = conv_pool.tile([P, CHUNK * K_PASS], U32, name="conv_words", align_bytes=64)
+            cols = slice(c * CHUNK * K_PASS, (c + 1) * CHUNK * K_PASS)
+            nc.sync.dma_start(
+                out=conv_words[c][:].bitcast(I32),
+                in_=conv_w_words[0, :, cols, :].rearrange("p n t -> p (n t)").bitcast(I32),
+            )
+
+        def load_heads(c):
+            groups = slice(c * CHUNK, (c + 1) * CHUNK)
+            cls_words[c] = head_pool.tile([P, CHUNK, CLS_COLS], U32, name="cls_words", align_bytes=64)
+            nc.sync.dma_start(
+                out=cls_words[c][:].bitcast(I32),
+                in_=cls_w_words[groups].rearrange("g p n t -> p g (n t)").bitcast(I32),
+            )
+            box_words[c] = head_pool.tile([P, CHUNK, BOX_COLS], U32, name="box_words", align_bytes=64)
+            nc.sync.dma_start(
+                out=box_words[c][:].bitcast(I32),
+                in_=bbox_w_words[groups, :, BOX_SKIP:, :].rearrange("g p n t -> p g (n t)").bitcast(I32),
+            )
+
+        load_conv(0)
+        load_conv(1)
+
+        bias_row = keep.tile([P, CLS_COLS + BOX_COLS], BF16)
+        nc.vector.memset(bias_row[:], 0.0)
+        nc.scalar.dma_start(out=bias_row[0:1, 0:CLS_COLS], in_=cls_b.unsqueeze(0))
+        nc.scalar.dma_start(out=bias_row[0:1, CLS_COLS:], in_=bbox_b[BOX_SKIP:].unsqueeze(0))
+        roi_sb = keep.tile([BATCH, PROPOSALS * 4], BF16)
+        nc.scalar.dma_start(out=roi_sb[:], in_=roi.rearrange("b n f -> b (n f)"))
+
+        ident_bf = keep.tile([P, P], BF16)
+        make_identity(nc, ident_bf[:])
+        ident_f32 = keep.tile([P, P], F32)
+        make_identity(nc, ident_f32[:])
+        ones = keep.tile([P, P], BF16)
+        nc.gpsimd.memset(ones[:], 1.0)
+        table = keep.tile([P, 1], F32)
+        nc.vector.memset(table[:], 0.0)
+        nc.scalar.activation(out=table[:], in_=table[:], func=ACT.Exp)
+
+        def k_onto_partitions(rows_sb):
+            turned = turn_pool.tile([P, PACK, P], BF16, name="turned_bf", tag="turned")
+            for t in range(PACK):
+                nc.tensor.transpose(out=turned[:, t, :], in_=rows_sb[:, t:K_PASS:PACK], identity=ident_bf[:])
+            return turned
+
+        feat_turned = k_onto_partitions(feat_sb)
+        feat_grouped = keep.tile([P, BATCH, PACK], BF16, align_bytes=64)
+        nc.vector.tensor_copy(out=feat_grouped[:], in_=feat_turned[:].rearrange("p t b -> p b t"))
+        feat_words = keep.tile([P, BATCH], U32, align_bytes=64)
+        feat_plane = keep.tile([P, BATCH], U8, align_bytes=64)
+        nc.vector.quantize_mx(
+            out=feat_words[:].bitcast(FP8X4),
+            scales=feat_plane[:],
+            in_=feat_grouped[:].rearrange("p b t -> p (b t)"),
+        )
+
+        conv_b_turned = k_onto_partitions(conv_b_rows)
+        conv_bias = keep.tile([P, GROUPS, PACK], F32)
+        nc.vector.tensor_copy(out=conv_bias[:], in_=conv_b_turned[:, :, 0:GROUPS].rearrange("p t g -> p g t"))
+
+        head_bias = keep.tile([BATCH, CLS_COLS + BOX_COLS], F32)
+        for first in range(0, CLS_COLS + BOX_COLS, 512):
+            width = min(512, CLS_COLS + BOX_COLS - first)
+            cols = slice(first, first + width)
+            spread = turn_pool.tile([P, 512], F32, name="spread", tag="turned")
+            nc.tensor.matmul(out=spread[:, 0:width], lhsT=ones[:], rhs=bias_row[:, cols], start=True, stop=True)
+            nc.scalar.copy(out=head_bias[:, cols], in_=spread[:, 0:width])
+        bias_c0 = head_bias[:, 0:PROPOSALS]
+        bias_c1 = head_bias[:, PROPOSALS:CLS_COLS]
+        bias_b1 = head_bias[:, CLS_COLS : CLS_COLS + PROPOSALS]
+        bias_b23 = head_bias[:, CLS_COLS + PROPOSALS :]
+
+        r = keep.tile([BATCH, 4, PROPOSALS], F32)
+        nc.vector.tensor_scalar_mul(out=r[:], in0=roi_sb[:].rearrange("b (n f) -> b f n", f=4), scalar1=STRIDE)
+        results = keep.tile([BATCH, 5, PROPOSALS], F32)
+        nc.vector.tensor_copy(out=results[:, 1, :], in_=r[:, 1, :])
+        x_early = keep.tile([BATCH, PROPOSALS], F32)
+        nc.vector.tensor_tensor(out=x_early[:], in0=bias_b1, in1=r[:, 3, :], op=ALU.mult)
+        nc.vector.tensor_tensor(out=x_early[:], in0=r[:, 0, :], in1=x_early[:], op=ALU.subtract)
+        bias_diff = keep.tile([BATCH, PROPOSALS], F32)
+        nc.vector.tensor_tensor(out=bias_diff[:], in0=bias_c1, in1=bias_c0, op=ALU.subtract)
+
+        acc_cls = acc_pool.tile([BATCH, CLS_COLS], F32)
+        acc_b23 = acc_pool.tile([BATCH, 2 * PROPOSALS], F32)
+        acc_b1 = acc_pool.tile([BATCH, PROPOSALS], F32)
+        sorted_sums = {}
+        flat_words = {}
+        flat_planes = {}
+
+        def conv_pass(c, i):
+            g = c * CHUNK + i
+            plane = g // (GROUPS // CHUNK)
+            first = (g % (GROUPS // CHUNK)) * K_PASS
+            sums = sums_pool.tile([BATCH, K_PASS], F32)
+            nc.tensor.matmul_mx(
+                out=sums[:],
+                lhsT=feat_words[:].bitcast(FP8X4),
+                lhsT_scale=feat_plane[:],
+                rhs=conv_words[c][:, i * K_PASS : (i + 1) * K_PASS].bitcast(FP8X4),
+                rhs_scale=conv_planes[4 * plane : P, first : first + K_PASS],
+                start=True,
+                stop=True,
+            )
+            nc.scalar.copy(out=sorted_sums[c][:, i, :, :], in_=sums[:].rearrange("b (p t) -> b t p", t=PACK))
+
+        def quantise_hidden(c):
+            turned = [turn_pool.tile([P, PACK, BATCH], F32, name="turned%d" % i, tag="turned") for i in range(CHUNK)]
+            for i in range(CHUNK):
+                for t in range(PACK):
+                    nc.tensor.transpose(out=turned[i][:, t, :], in_=sorted_sums[c][:, i, t, :], identity=ident_f32[:])
+            hidden = work.tile([P, CHUNK, BATCH, PACK], BF16, align_bytes=64)
+            for i in range(CHUNK):
+                nc.vector.tensor_tensor(
+                    out=hidden[:, i, :, :],
+                    in0=turned[i][:].rearrange("p t b -> p b t"),
+                    in1=conv_bias[:, c * CHUNK + i, :].unsqueeze(1).to_broadcast([P, BATCH, PACK]),
+                    op=ALU.add,
+                )
+            hidden_flat = hidden[:].rearrange("p i b t -> p (i b t)")
+            nc.vector.tensor_scalar_max(out=hidden_flat, in0=hidden_flat, scalar1=0.0)
+            flat_words[c] = work.tile([P, CHUNK, BATCH], U32, name="flat_words", align_bytes=64)
+            flat_planes[c] = work.tile([P, CHUNK, BATCH], U8, name="flat_planes", align_bytes=64)
+            nc.vector.quantize_mx(
+                out=flat_words[c][:].rearrange("p i b -> p (i b)").bitcast(FP8X4),
+                scales=flat_planes[c][:].rearrange("p i b -> p (i b)"),
+                in_=hidden_flat,
+            )
+
+        def head_passes(c, i):
+            g = c * CHUNK + i
+            for acc, words, planes in (
+                (acc_cls, cls_words[c][:, i, :], cls_planes[4 * i : P, c, :]),
+                (acc_b23, box_words[c][:, i, PROPOSALS:], box_planes[4 * i : P, c, PROPOSALS:]),
+                (acc_b1, box_words[c][:, i, 0:PROPOSALS], box_planes[4 * i : P, c, 0:PROPOSALS]),
+            ):
+                nc.tensor.matmul_mx(
+                    out=acc[:],
+                    lhsT=flat_words[c][:, i, :].bitcast(FP8X4),
+                    lhsT_scale=flat_planes[c][:, i, :],
+                    rhs=words.bitcast(FP8X4),
+                    rhs_scale=planes,
+                    start=(g == 0),
+                    stop=(g == GROUPS - 1),
+                )
+
+        for s in range(CHUNKS + 2):
+            if s + 2 < CHUNKS:
+                load_conv(s + 2)
+            if s < CHUNKS:
+                load_heads(s)
+                sorted_sums[s] = work.tile([BATCH, CHUNK, PACK, P], F32, name="sorted_sums")
+            if 1 <= s <= CHUNKS:
+                quantise_hidden(s - 1)
+            for i in range(CHUNK):
+                if s < CHUNKS:
+                    conv_pass(s, i)
+                if s >= 2:
+                    head_passes(s - 2, i)
+
+        logit = keep.tile([BATCH, PROPOSALS], F32)
+        nc.vector.tensor_tensor(out=logit[:], in0=acc_cls[:, PROPOSALS:], in1=bias_diff[:], op=ALU.add)
+        nc.vector.tensor_tensor(out=logit[:], in0=logit[:], in1=acc_cls[:, 0:PROPOSALS], op=ALU.subtract)
+        nc.scalar.activation(out=logit[:], in_=logit[:], func=ACT.Tanh, scale=0.5)
+        nc.vector.tensor_scalar(
+            out=results[:, 4, :], in0=logit[:], scalar1=0.5, scalar2=0.5, op0=ALU.mult, op1=ALU.add
+        )
+        growth = keep.tile([BATCH, 2 * PROPOSALS], F32)
+        nc.vector.tensor_tensor(out=growth[:], in0=acc_b23[:], in1=bias_b23, op=ALU.add)
+        nc.vector.tensor_scalar(out=growth[:], in0=growth[:], scalar1=CLIP, scalar2=-CLIP, op0=ALU.min, op1=ALU.max)
+        nc.scalar.activation(out=growth[:], in_=growth[:], func=ACT.Exp)
+        shift = keep.tile([BATCH, PROPOSALS], F32)
+        nc.vector.tensor_tensor(out=shift[:], in0=acc_b1[:], in1=r[:, 3, :], op=ALU.mult)
+        nc.vector.tensor_tensor(out=results[:, 0, :], in0=x_early[:], in1=shift[:], op=ALU.subtract)
+        nc.vector.tensor_tensor(
+            out=results[:, 2:4, :].rearrange("b f n -> b (f n)"),
+            in0=r[:, 2:4, :].rearrange("b f n -> b (f n)"),
+            in1=growth[:],
+            op=ALU.mult,
+        )
+        out_sb = keep.tile([BATCH, PROPOSALS, 5], F32)
+        half = PROPOSALS // 2
+        nc.vector.tensor_copy(out=out_sb[:, 0:half, :], in_=results[:, :, 0:half].rearrange("b f n -> b n f"))
+        nc.sync.dma_start(out=out[:, 0:half, :], in_=out_sb[:, 0:half, :])
+        nc.scalar.copy(out=out_sb[:, half:, :], in_=results[:, :, half:].rearrange("b f n -> b n f"))
+        nc.sync.dma_start(out=out[:, half:, :], in_=out_sb[:, half:, :])

@@ -26,6 +26,7 @@ GROUPS = HIDDEN // K_PASS
 CHUNK = 4
 CHUNKS = GROUPS // CHUNK
 QUADS = 4
+HEAD_LAG = 5
 STRIDE = 16.0
 CLIP = 10.0
 
@@ -55,12 +56,20 @@ def tile_classifiermodel_k_kernel(
     nc = tc.nc
     with ExitStack() as stack:
         keep = stack.enter_context(tc.tile_pool(name="keep", bufs=1))
-        conv_pool = stack.enter_context(tc.tile_pool(name="conv", bufs=3))
+        conv_pool = stack.enter_context(tc.tile_pool(name="conv", bufs=6))
         head_pool = stack.enter_context(tc.tile_pool(name="heads", bufs=4))
         work = stack.enter_context(tc.tile_pool(name="work", bufs=2))
+        flat_pool = stack.enter_context(tc.tile_pool(name="flat", bufs=HEAD_LAG + 1))
         acc_pool = stack.enter_context(tc.psum_pool(name="acc", bufs=1))
-        turn_pool = stack.enter_context(tc.psum_pool(name="turn", bufs=CHUNK))
-        sums_pool = stack.enter_context(tc.psum_pool(name="sums", bufs=1))
+        turn_pool = stack.enter_context(tc.psum_pool(name="turn", bufs=3))
+        sums_pool = stack.enter_context(tc.psum_pool(name="sums", bufs=2))
+
+        ident_bf = keep.tile([P, P], BF16)
+        make_identity(nc, ident_bf[:])
+        ident_f32 = keep.tile([P, P], F32)
+        make_identity(nc, ident_f32[:])
+        ones = keep.tile([P, P], BF16)
+        nc.gpsimd.memset(ones[:], 1.0)
 
         feat_sb = keep.tile([BATCH, CHANNELS], BF16)
         nc.scalar.dma_start(out=feat_sb[:], in_=features.rearrange("b h w c -> b (h w c)"))
@@ -72,27 +81,20 @@ def tile_classifiermodel_k_kernel(
         cls_planes = keep.tile([P, CHUNKS, CLS_COLS], U8, align_bytes=64)
         box_planes = keep.tile([P, CHUNKS, BOX_COLS], U8, align_bytes=64)
         nc.vector.memset(conv_planes[:].bitcast(I32), 0)
-        nc.vector.memset(cls_planes[:].bitcast(I32), 0)
         nc.vector.memset(box_planes[:].bitcast(I32), 0)
+        nc.vector.memset(cls_planes[:].bitcast(I32), 0)
         for quad in range(QUADS):
             nc.sync.dma_start(
                 out=conv_planes[32 * quad : 32 * quad + 16, :].bitcast(I32),
                 in_=conv_w_scales[0, 4 * quad : 4 * quad + 4, :].rearrange("r (i n) -> i r n", i=CHUNK).bitcast(I32),
             )
-        for quad in range(QUADS):
-            for r in range(4):
-                rows = slice(32 * quad + r, 32 * quad + 16, 4)
-                nc.sync.dma_start(
-                    out=cls_planes[rows, :, :].bitcast(I32),
-                    in_=cls_w_scales[:, 4 * quad + r, :].rearrange("(c i) n -> i c n", i=CHUNK).bitcast(I32),
-                )
-        for quad in range(QUADS):
-            for r in range(4):
-                rows = slice(32 * quad + r, 32 * quad + 16, 4)
-                nc.sync.dma_start(
-                    out=box_planes[rows, :, :].bitcast(I32),
-                    in_=bbox_w_scales[:, 4 * quad + r, BOX_SKIP:].rearrange("(c i) n -> i c n", i=CHUNK).bitcast(I32),
-                )
+        for planes, scales in ((box_planes, bbox_w_scales[:, :, BOX_SKIP:]), (cls_planes, cls_w_scales)):
+            for quad in range(QUADS):
+                for r in range(4):
+                    nc.gpsimd.dma_start(
+                        out=planes[32 * quad + r : 32 * quad + 16 : 4, :, :].bitcast(F32),
+                        in_=scales[:, 4 * quad + r, :].rearrange("(c i) n -> i c n", i=CHUNK).bitcast(F32),
+                    )
 
         conv_words = {}
         cls_words = {}
@@ -107,20 +109,22 @@ def tile_classifiermodel_k_kernel(
             )
 
         def load_heads(c):
-            groups = slice(c * CHUNK, (c + 1) * CHUNK)
-            cls_words[c] = head_pool.tile([P, CHUNK, CLS_COLS], U32, name="cls_words", align_bytes=64)
-            nc.sync.dma_start(
-                out=cls_words[c][:].bitcast(I32),
-                in_=cls_w_words[groups].rearrange("g p n t -> p g (n t)").bitcast(I32),
-            )
+            first = c * CHUNK
             box_words[c] = head_pool.tile([P, CHUNK, BOX_COLS], U32, name="box_words", align_bytes=64)
             nc.sync.dma_start(
                 out=box_words[c][:].bitcast(I32),
-                in_=bbox_w_words[groups, :, BOX_SKIP:, :].rearrange("g p n t -> p g (n t)").bitcast(I32),
+                in_=bbox_w_words[first : first + CHUNK, :, BOX_SKIP:, :].rearrange("g p n t -> p g (n t)").bitcast(I32),
             )
+            cls_words[c] = head_pool.tile([P, CHUNK, CLS_COLS], U32, name="cls_words", align_bytes=64)
+            groups_a_load = 1 if c == CHUNKS - 1 else CHUNK
+            for i in range(0, CHUNK, groups_a_load):
+                nc.sync.dma_start(
+                    out=cls_words[c][:, i : i + groups_a_load, :].bitcast(I32),
+                    in_=cls_w_words[first + i : first + i + groups_a_load].rearrange("g p n t -> p g (n t)").bitcast(I32),
+                )
 
-        load_conv(0)
-        load_conv(1)
+        for c in range(CHUNKS):
+            load_conv(c)
 
         bias_row = keep.tile([P, CLS_COLS + BOX_COLS], BF16)
         nc.vector.memset(bias_row[:], 0.0)
@@ -128,13 +132,6 @@ def tile_classifiermodel_k_kernel(
         nc.scalar.dma_start(out=bias_row[0:1, CLS_COLS:], in_=bbox_b[BOX_SKIP:].unsqueeze(0))
         roi_sb = keep.tile([BATCH, PROPOSALS * 4], BF16)
         nc.scalar.dma_start(out=roi_sb[:], in_=roi.rearrange("b n f -> b (n f)"))
-
-        ident_bf = keep.tile([P, P], BF16)
-        make_identity(nc, ident_bf[:])
-        ident_f32 = keep.tile([P, P], F32)
-        make_identity(nc, ident_f32[:])
-        ones = keep.tile([P, P], BF16)
-        nc.gpsimd.memset(ones[:], 1.0)
         table = keep.tile([P, 1], F32)
         nc.vector.memset(table[:], 0.0)
         nc.scalar.activation(out=table[:], in_=table[:], func=ACT.Exp)
@@ -206,66 +203,57 @@ def tile_classifiermodel_k_kernel(
             nc.scalar.copy(out=sorted_sums[c][:, i, :, :], in_=sums[:].rearrange("b (p t) -> b t p", t=PACK))
 
         def quantise_hidden(c):
-            turned = [turn_pool.tile([P, PACK, BATCH], F32, name="turned%d" % i, tag="turned") for i in range(CHUNK)]
-            for i in range(CHUNK):
-                for t in range(PACK):
-                    nc.tensor.transpose(out=turned[i][:, t, :], in_=sorted_sums[c][:, i, t, :], identity=ident_f32[:])
             hidden = work.tile([P, CHUNK, BATCH, PACK], BF16, align_bytes=64)
             for i in range(CHUNK):
+                turned = turn_pool.tile([P, PACK, BATCH], F32)
+                for t in range(PACK):
+                    nc.tensor.transpose(out=turned[:, t, :], in_=sorted_sums[c][:, i, t, :], identity=ident_f32[:])
                 nc.vector.tensor_tensor(
                     out=hidden[:, i, :, :],
-                    in0=turned[i][:].rearrange("p t b -> p b t"),
+                    in0=turned[:].rearrange("p t b -> p b t"),
                     in1=conv_bias[:, c * CHUNK + i, :].unsqueeze(1).to_broadcast([P, BATCH, PACK]),
                     op=ALU.add,
                 )
             hidden_flat = hidden[:].rearrange("p i b t -> p (i b t)")
             nc.vector.tensor_scalar_max(out=hidden_flat, in0=hidden_flat, scalar1=0.0)
-            flat_words[c] = work.tile([P, CHUNK, BATCH], U32, name="flat_words", align_bytes=64)
-            flat_planes[c] = work.tile([P, CHUNK, BATCH], U8, name="flat_planes", align_bytes=64)
+            flat_words[c] = flat_pool.tile([P, CHUNK, BATCH], U32, name="flat_words", align_bytes=64)
+            flat_planes[c] = flat_pool.tile([P, CHUNK, BATCH], U8, name="flat_planes", align_bytes=64)
             nc.vector.quantize_mx(
                 out=flat_words[c][:].rearrange("p i b -> p (i b)").bitcast(FP8X4),
                 scales=flat_planes[c][:].rearrange("p i b -> p (i b)"),
                 in_=hidden_flat,
             )
 
-        def head_passes(c, i):
+        def head_pass(acc, c, i, words, plane):
             g = c * CHUNK + i
-            for acc, words, planes in (
-                (acc_cls, cls_words[c][:, i, :], cls_planes[4 * i : P, c, :]),
-                (acc_b23, box_words[c][:, i, PROPOSALS:], box_planes[4 * i : P, c, PROPOSALS:]),
-                (acc_b1, box_words[c][:, i, 0:PROPOSALS], box_planes[4 * i : P, c, 0:PROPOSALS]),
-            ):
-                nc.tensor.matmul_mx(
-                    out=acc[:],
-                    lhsT=flat_words[c][:, i, :].bitcast(FP8X4),
-                    lhsT_scale=flat_planes[c][:, i, :],
-                    rhs=words.bitcast(FP8X4),
-                    rhs_scale=planes,
-                    start=(g == 0),
-                    stop=(g == GROUPS - 1),
-                )
+            nc.tensor.matmul_mx(
+                out=acc[:],
+                lhsT=flat_words[c][:, i, :].bitcast(FP8X4),
+                lhsT_scale=flat_planes[c][:, i, :],
+                rhs=words.bitcast(FP8X4),
+                rhs_scale=plane,
+                start=(g == 0),
+                stop=(g == GROUPS - 1),
+            )
 
-        for s in range(CHUNKS + 2):
-            if s + 2 < CHUNKS:
-                load_conv(s + 2)
+        for s in range(CHUNKS + HEAD_LAG):
+            c = s - HEAD_LAG
+            if 0 <= c + 2 < CHUNKS:
+                load_heads(c + 2)
             if s < CHUNKS:
-                load_heads(s)
                 sorted_sums[s] = work.tile([BATCH, CHUNK, PACK, P], F32, name="sorted_sums")
             if 1 <= s <= CHUNKS:
                 quantise_hidden(s - 1)
             for i in range(CHUNK):
                 if s < CHUNKS:
                     conv_pass(s, i)
-                if s >= 2:
-                    head_passes(s - 2, i)
+                if c >= 0:
+                    head_pass(acc_b23, c, i, box_words[c][:, i, PROPOSALS:], box_planes[4 * i : P, c, PROPOSALS:])
+                    head_pass(acc_b1, c, i, box_words[c][:, i, 0:PROPOSALS], box_planes[4 * i : P, c, 0:PROPOSALS])
+            for i in range(CHUNK):
+                if c >= 0:
+                    head_pass(acc_cls, c, i, cls_words[c][:, i, :], cls_planes[4 * i : P, c, :])
 
-        logit = keep.tile([BATCH, PROPOSALS], F32)
-        nc.vector.tensor_tensor(out=logit[:], in0=acc_cls[:, PROPOSALS:], in1=bias_diff[:], op=ALU.add)
-        nc.vector.tensor_tensor(out=logit[:], in0=logit[:], in1=acc_cls[:, 0:PROPOSALS], op=ALU.subtract)
-        nc.scalar.activation(out=logit[:], in_=logit[:], func=ACT.Tanh, scale=0.5)
-        nc.vector.tensor_scalar(
-            out=results[:, 4, :], in0=logit[:], scalar1=0.5, scalar2=0.5, op0=ALU.mult, op1=ALU.add
-        )
         growth = keep.tile([BATCH, 2 * PROPOSALS], F32)
         nc.vector.tensor_tensor(out=growth[:], in0=acc_b23[:], in1=bias_b23, op=ALU.add)
         nc.vector.tensor_scalar(out=growth[:], in0=growth[:], scalar1=CLIP, scalar2=-CLIP, op0=ALU.min, op1=ALU.max)
@@ -279,9 +267,16 @@ def tile_classifiermodel_k_kernel(
             in1=growth[:],
             op=ALU.mult,
         )
+        logit = keep.tile([BATCH, PROPOSALS], F32)
+        nc.vector.tensor_tensor(out=logit[:], in0=acc_cls[:, PROPOSALS:], in1=bias_diff[:], op=ALU.add)
+        nc.vector.tensor_tensor(out=logit[:], in0=logit[:], in1=acc_cls[:, 0:PROPOSALS], op=ALU.subtract)
+        nc.scalar.activation(out=logit[:], in_=logit[:], func=ACT.Tanh, scale=0.5)
+        nc.vector.tensor_scalar(
+            out=results[:, 4, :], in0=logit[:], scalar1=0.5, scalar2=0.5, op0=ALU.mult, op1=ALU.add
+        )
         out_sb = keep.tile([BATCH, PROPOSALS, 5], F32)
-        half = PROPOSALS // 2
-        nc.vector.tensor_copy(out=out_sb[:, 0:half, :], in_=results[:, :, 0:half].rearrange("b f n -> b n f"))
-        nc.sync.dma_start(out=out[:, 0:half, :], in_=out_sb[:, 0:half, :])
-        nc.scalar.copy(out=out_sb[:, half:, :], in_=results[:, :, half:].rearrange("b f n -> b n f"))
-        nc.sync.dma_start(out=out[:, half:, :], in_=out_sb[:, half:, :])
+        cut = 168
+        nc.scalar.copy(out=out_sb[:, cut:, :], in_=results[:, :, cut:].rearrange("b f n -> b n f"))
+        nc.vector.tensor_copy(out=out_sb[:, 0:cut, :], in_=results[:, :, 0:cut].rearrange("b f n -> b n f"))
+        nc.sync.dma_start(out=out[:, 0:cut, :], in_=out_sb[:, 0:cut, :])
+        nc.sync.dma_start(out=out[:, cut:, :], in_=out_sb[:, cut:, :])

@@ -55,6 +55,7 @@ def tile_classifiermodel_k_kernel(
 ):
     nc = tc.nc
     with ExitStack() as stack:
+        stack.enter_context(tc.manual_schedule())
         keep = stack.enter_context(tc.tile_pool(name="keep", bufs=1))
         conv_pool = stack.enter_context(tc.tile_pool(name="conv", bufs=6))
         head_pool = stack.enter_context(tc.tile_pool(name="heads", bufs=4))
@@ -158,26 +159,27 @@ def tile_classifiermodel_k_kernel(
         nc.vector.tensor_copy(out=conv_bias[:], in_=conv_b_turned[:, :, 0:GROUPS].rearrange("p t g -> p g t"))
 
         head_bias = keep.tile([BATCH, CLS_COLS + BOX_COLS], F32)
-        for first in range(0, CLS_COLS + BOX_COLS, 512):
-            width = min(512, CLS_COLS + BOX_COLS - first)
-            cols = slice(first, first + width)
-            spread = turn_pool.tile([P, 512], F32, name="spread", tag="turned")
-            nc.tensor.matmul(out=spread[:, 0:width], lhsT=ones[:], rhs=bias_row[:, cols], start=True, stop=True)
-            nc.scalar.copy(out=head_bias[:, cols], in_=spread[:, 0:width])
         bias_c0 = head_bias[:, 0:PROPOSALS]
         bias_c1 = head_bias[:, PROPOSALS:CLS_COLS]
         bias_b1 = head_bias[:, CLS_COLS : CLS_COLS + PROPOSALS]
         bias_b23 = head_bias[:, CLS_COLS + PROPOSALS :]
-
         r = keep.tile([BATCH, 4, PROPOSALS], F32)
-        nc.vector.tensor_scalar_mul(out=r[:], in0=roi_sb[:].rearrange("b (n f) -> b f n", f=4), scalar1=STRIDE)
         results = keep.tile([BATCH, 5, PROPOSALS], F32)
-        nc.vector.tensor_copy(out=results[:, 1, :], in_=r[:, 1, :])
         x_early = keep.tile([BATCH, PROPOSALS], F32)
-        nc.vector.tensor_tensor(out=x_early[:], in0=bias_b1, in1=r[:, 3, :], op=ALU.mult)
-        nc.vector.tensor_tensor(out=x_early[:], in0=r[:, 0, :], in1=x_early[:], op=ALU.subtract)
         bias_diff = keep.tile([BATCH, PROPOSALS], F32)
-        nc.vector.tensor_tensor(out=bias_diff[:], in0=bias_c1, in1=bias_c0, op=ALU.subtract)
+
+        def prepare_end():
+            for first in range(0, CLS_COLS + BOX_COLS, 512):
+                width = min(512, CLS_COLS + BOX_COLS - first)
+                cols = slice(first, first + width)
+                spread = turn_pool.tile([P, 512], F32, name="spread", tag="turned")
+                nc.tensor.matmul(out=spread[:, 0:width], lhsT=ones[:], rhs=bias_row[:, cols], start=True, stop=True)
+                nc.scalar.copy(out=head_bias[:, cols], in_=spread[:, 0:width])
+            nc.vector.tensor_scalar_mul(out=r[:], in0=roi_sb[:].rearrange("b (n f) -> b f n", f=4), scalar1=STRIDE)
+            nc.vector.tensor_copy(out=results[:, 1, :], in_=r[:, 1, :])
+            nc.vector.tensor_tensor(out=x_early[:], in0=bias_b1, in1=r[:, 3, :], op=ALU.mult)
+            nc.vector.tensor_tensor(out=x_early[:], in0=r[:, 0, :], in1=x_early[:], op=ALU.subtract)
+            nc.vector.tensor_tensor(out=bias_diff[:], in0=bias_c1, in1=bias_c0, op=ALU.subtract)
 
         acc_cls = acc_pool.tile([BATCH, CLS_COLS], F32)
         acc_b23 = acc_pool.tile([BATCH, 2 * PROPOSALS], F32)
@@ -238,6 +240,8 @@ def tile_classifiermodel_k_kernel(
 
         for s in range(CHUNKS + HEAD_LAG):
             c = s - HEAD_LAG
+            if s == CHUNKS + 1:
+                prepare_end()
             if 0 <= c + 2 < CHUNKS:
                 load_heads(c + 2)
             if s < CHUNKS:

@@ -26,7 +26,9 @@ GROUPS = HIDDEN // K_PASS
 CHUNK = 4
 CHUNKS = GROUPS // CHUNK
 QUADS = 4
-HEAD_LAG = 5
+BOX_LAG = 5
+BOX_BUFS = 6
+assert CHUNKS - 1 - BOX_BUFS + BOX_LAG < CHUNKS - 1
 STRIDE = 16.0
 CLIP = 10.0
 
@@ -57,37 +59,76 @@ def tile_classifiermodel_k_kernel(
     with ExitStack() as stack:
         stack.enter_context(tc.manual_schedule())
         keep = stack.enter_context(tc.tile_pool(name="keep", bufs=1))
-        conv_pool = stack.enter_context(tc.tile_pool(name="conv", bufs=6))
-        head_pool = stack.enter_context(tc.tile_pool(name="heads", bufs=4))
+        wide_pool = stack.enter_context(tc.tile_pool(name="wide", bufs=CHUNKS))
+        box_pool = stack.enter_context(tc.tile_pool(name="box", bufs=BOX_BUFS))
         work = stack.enter_context(tc.tile_pool(name="work", bufs=2))
-        flat_pool = stack.enter_context(tc.tile_pool(name="flat", bufs=HEAD_LAG + 1))
+        flat_pool = stack.enter_context(tc.tile_pool(name="flat", bufs=CHUNKS))
         acc_pool = stack.enter_context(tc.psum_pool(name="acc", bufs=1))
         turn_pool = stack.enter_context(tc.psum_pool(name="turn", bufs=3))
         sums_pool = stack.enter_context(tc.psum_pool(name="sums", bufs=2))
 
+        conv_words = {}
+        cls_words = {}
+        box_words = {}
+
+        def load_conv(c):
+            conv_words[c] = wide_pool.tile([P, CHUNK * K_PASS], U32, name="conv_words", tag="wide", align_bytes=64)
+            cols = slice(c * CHUNK * K_PASS, (c + 1) * CHUNK * K_PASS)
+            nc.sync.dma_start(
+                out=conv_words[c][:].bitcast(I32),
+                in_=conv_w_words[0, :, cols, :].rearrange("p n t -> p (n t)").bitcast(I32),
+            )
+
+        def load_box(c):
+            first = c * CHUNK
+            box_words[c] = box_pool.tile([P, CHUNK, BOX_COLS], U32, name="box_words", align_bytes=64)
+            for i in range(0, CHUNK, 2):
+                nc.sync.dma_start(
+                    out=box_words[c][:, i : i + 2, :].bitcast(I32),
+                    in_=bbox_w_words[first + i : first + i + 2, :, BOX_SKIP:, :]
+                    .rearrange("g p n t -> p g (n t)")
+                    .bitcast(I32),
+                )
+
+        def load_cls(c):
+            first = c * CHUNK
+            cls_words[c] = wide_pool.tile([P, CHUNK, CLS_COLS], U32, name="cls_words", tag="wide", align_bytes=64)
+            groups_a_load = 1 if c == CHUNKS - 1 else 2
+            for i in range(0, CHUNK, groups_a_load):
+                nc.sync.dma_start(
+                    out=cls_words[c][:, i : i + groups_a_load, :].bitcast(I32),
+                    in_=cls_w_words[first + i : first + i + groups_a_load].rearrange("g p n t -> p g (n t)").bitcast(I32),
+                )
+
+        load_conv(0)
         ident_bf = keep.tile([P, P], BF16)
         make_identity(nc, ident_bf[:])
-        ident_f32 = keep.tile([P, P], F32)
-        make_identity(nc, ident_f32[:])
-        ones = keep.tile([P, P], BF16)
-        nc.gpsimd.memset(ones[:], 1.0)
-
         feat_sb = keep.tile([BATCH, CHANNELS], BF16)
         nc.scalar.dma_start(out=feat_sb[:], in_=features.rearrange("b h w c -> b (h w c)"))
-        conv_b_rows = keep.tile([P, K_PASS], BF16)
-        nc.vector.memset(conv_b_rows[:], 0.0)
-        nc.scalar.dma_start(out=conv_b_rows[0:GROUPS, :], in_=conv_b.rearrange("(g k) -> g k", k=K_PASS))
 
         conv_planes = keep.tile([P, HIDDEN // CHUNK], U8, align_bytes=64)
         cls_planes = keep.tile([P, CHUNKS, CLS_COLS], U8, align_bytes=64)
         box_planes = keep.tile([P, CHUNKS, BOX_COLS], U8, align_bytes=64)
+        conv_b_rows = keep.tile([P, K_PASS], BF16)
+        bias_row = keep.tile([P, CLS_COLS + BOX_COLS], BF16)
+        table = keep.tile([P, 1], F32)
         nc.vector.memset(conv_planes[:].bitcast(I32), 0)
+        nc.vector.memset(conv_b_rows[:], 0.0)
+        nc.vector.memset(bias_row[:], 0.0)
+        nc.vector.memset(table[:], 0.0)
         nc.vector.memset(box_planes[:].bitcast(I32), 0)
         nc.vector.memset(cls_planes[:].bitcast(I32), 0)
+        nc.scalar.dma_start(out=conv_b_rows[0:GROUPS, :], in_=conv_b.rearrange("(g k) -> g k", k=K_PASS))
+        nc.scalar.dma_start(out=bias_row[0:1, 0:CLS_COLS], in_=cls_b.unsqueeze(0))
+        nc.scalar.dma_start(out=bias_row[0:1, CLS_COLS:], in_=bbox_b[BOX_SKIP:].unsqueeze(0))
+        roi_sb = keep.tile([BATCH, PROPOSALS * 4], BF16)
+        nc.scalar.dma_start(out=roi_sb[:], in_=roi.rearrange("b n f -> b (n f)"))
+        nc.scalar.activation(out=table[:], in_=table[:], func=ACT.Exp)
+
         for quad in range(QUADS):
-            nc.sync.dma_start(
-                out=conv_planes[32 * quad : 32 * quad + 16, :].bitcast(I32),
-                in_=conv_w_scales[0, 4 * quad : 4 * quad + 4, :].rearrange("r (i n) -> i r n", i=CHUNK).bitcast(I32),
+            nc.gpsimd.dma_start(
+                out=conv_planes[32 * quad : 32 * quad + 16, :].bitcast(F32),
+                in_=conv_w_scales[0, 4 * quad : 4 * quad + 4, :].rearrange("r (i n) -> i r n", i=CHUNK).bitcast(F32),
             )
         for planes, scales in ((box_planes, bbox_w_scales[:, :, BOX_SKIP:]), (cls_planes, cls_w_scales)):
             for quad in range(QUADS):
@@ -97,45 +138,15 @@ def tile_classifiermodel_k_kernel(
                         in_=scales[:, 4 * quad + r, :].rearrange("(c i) n -> i c n", i=CHUNK).bitcast(F32),
                     )
 
-        conv_words = {}
-        cls_words = {}
-        box_words = {}
-
-        def load_conv(c):
-            conv_words[c] = conv_pool.tile([P, CHUNK * K_PASS], U32, name="conv_words", align_bytes=64)
-            cols = slice(c * CHUNK * K_PASS, (c + 1) * CHUNK * K_PASS)
-            nc.sync.dma_start(
-                out=conv_words[c][:].bitcast(I32),
-                in_=conv_w_words[0, :, cols, :].rearrange("p n t -> p (n t)").bitcast(I32),
-            )
-
-        def load_heads(c):
-            first = c * CHUNK
-            box_words[c] = head_pool.tile([P, CHUNK, BOX_COLS], U32, name="box_words", align_bytes=64)
-            nc.sync.dma_start(
-                out=box_words[c][:].bitcast(I32),
-                in_=bbox_w_words[first : first + CHUNK, :, BOX_SKIP:, :].rearrange("g p n t -> p g (n t)").bitcast(I32),
-            )
-            cls_words[c] = head_pool.tile([P, CHUNK, CLS_COLS], U32, name="cls_words", align_bytes=64)
-            groups_a_load = 1 if c == CHUNKS - 1 else CHUNK
-            for i in range(0, CHUNK, groups_a_load):
-                nc.sync.dma_start(
-                    out=cls_words[c][:, i : i + groups_a_load, :].bitcast(I32),
-                    in_=cls_w_words[first + i : first + i + groups_a_load].rearrange("g p n t -> p g (n t)").bitcast(I32),
-                )
-
-        for c in range(CHUNKS):
+        for c in range(1, CHUNKS):
             load_conv(c)
+        for c in range(BOX_BUFS):
+            load_box(c)
 
-        bias_row = keep.tile([P, CLS_COLS + BOX_COLS], BF16)
-        nc.vector.memset(bias_row[:], 0.0)
-        nc.scalar.dma_start(out=bias_row[0:1, 0:CLS_COLS], in_=cls_b.unsqueeze(0))
-        nc.scalar.dma_start(out=bias_row[0:1, CLS_COLS:], in_=bbox_b[BOX_SKIP:].unsqueeze(0))
-        roi_sb = keep.tile([BATCH, PROPOSALS * 4], BF16)
-        nc.scalar.dma_start(out=roi_sb[:], in_=roi.rearrange("b n f -> b (n f)"))
-        table = keep.tile([P, 1], F32)
-        nc.vector.memset(table[:], 0.0)
-        nc.scalar.activation(out=table[:], in_=table[:], func=ACT.Exp)
+        ident_f32 = keep.tile([P, P], F32)
+        nc.vector.tensor_copy(out=ident_f32[:], in_=ident_bf[:])
+        ones = keep.tile([P, P], BF16)
+        nc.vector.memset(ones[:], 1.0)
 
         def k_onto_partitions(rows_sb):
             turned = turn_pool.tile([P, PACK, P], BF16, name="turned_bf", tag="turned")
@@ -238,25 +249,35 @@ def tile_classifiermodel_k_kernel(
                 stop=(g == GROUPS - 1),
             )
 
-        for s in range(CHUNKS + HEAD_LAG):
-            c = s - HEAD_LAG
-            if s == CHUNKS + 1:
-                prepare_end()
-            if 0 <= c + 2 < CHUNKS:
-                load_heads(c + 2)
+        def box_passes(c, i):
+            head_pass(acc_b23, c, i, box_words[c][:, i, PROPOSALS:], box_planes[4 * i : P, c, PROPOSALS:])
+            head_pass(acc_b1, c, i, box_words[c][:, i, 0:PROPOSALS], box_planes[4 * i : P, c, 0:PROPOSALS])
+
+        def after_box(c):
+            if c + BOX_BUFS < CHUNKS:
+                load_box(c + BOX_BUFS)
+
+        for s in range(CHUNKS + 1):
+            c = s - BOX_LAG
             if s < CHUNKS:
                 sorted_sums[s] = work.tile([BATCH, CHUNK, PACK, P], F32, name="sorted_sums")
-            if 1 <= s <= CHUNKS:
-                quantise_hidden(s - 1)
             for i in range(CHUNK):
                 if s < CHUNKS:
                     conv_pass(s, i)
                 if c >= 0:
-                    head_pass(acc_b23, c, i, box_words[c][:, i, PROPOSALS:], box_planes[4 * i : P, c, PROPOSALS:])
-                    head_pass(acc_b1, c, i, box_words[c][:, i, 0:PROPOSALS], box_planes[4 * i : P, c, 0:PROPOSALS])
+                    box_passes(c, i)
+            if c >= 0:
+                after_box(c)
+            if s == CHUNKS - 1:
+                for later in range(CHUNKS):
+                    load_cls(later)
+            if s >= 1:
+                quantise_hidden(s - 1)
+        prepare_end()
+        for c in range(CHUNKS + 1 - BOX_LAG, CHUNKS):
             for i in range(CHUNK):
-                if c >= 0:
-                    head_pass(acc_cls, c, i, cls_words[c][:, i, :], cls_planes[4 * i : P, c, :])
+                box_passes(c, i)
+            after_box(c)
 
         growth = keep.tile([BATCH, 2 * PROPOSALS], F32)
         nc.vector.tensor_tensor(out=growth[:], in0=acc_b23[:], in1=bias_b23, op=ALU.add)
@@ -271,6 +292,10 @@ def tile_classifiermodel_k_kernel(
             in1=growth[:],
             op=ALU.mult,
         )
+
+        for c in range(CHUNKS):
+            for i in range(CHUNK):
+                head_pass(acc_cls, c, i, cls_words[c][:, i, :], cls_planes[4 * i : P, c, :])
         logit = keep.tile([BATCH, PROPOSALS], F32)
         nc.vector.tensor_tensor(out=logit[:], in0=acc_cls[:, PROPOSALS:], in1=bias_diff[:], op=ALU.add)
         nc.vector.tensor_tensor(out=logit[:], in0=logit[:], in1=acc_cls[:, 0:PROPOSALS], op=ALU.subtract)

@@ -29,6 +29,7 @@ QUADS = 4
 BOX_LAG = 5
 BOX_BUFS = 6
 assert CHUNKS - 1 - BOX_BUFS + BOX_LAG < CHUNKS - 1
+HALF = PROPOSALS // 2
 STRIDE = 16.0
 CLIP = 10.0
 
@@ -175,7 +176,7 @@ def tile_classifiermodel_k_kernel(
         bias_b1 = head_bias[:, CLS_COLS : CLS_COLS + PROPOSALS]
         bias_b23 = head_bias[:, CLS_COLS + PROPOSALS :]
         r = keep.tile([BATCH, 4, PROPOSALS], F32)
-        results = keep.tile([BATCH, 5, PROPOSALS], F32)
+        results = keep.tile([BATCH, 4, PROPOSALS], F32)
         x_early = keep.tile([BATCH, PROPOSALS], F32)
         bias_diff = keep.tile([BATCH, PROPOSALS], F32)
 
@@ -292,20 +293,22 @@ def tile_classifiermodel_k_kernel(
             in1=growth[:],
             op=ALU.mult,
         )
+        out_sb = keep.tile([BATCH, PROPOSALS, 5], F32)
+        nc.vector.tensor_copy(out=out_sb[:, :, 0:4], in_=results[:].rearrange("b f n -> b n f"))
 
         for c in range(CHUNKS):
             for i in range(CHUNK):
                 head_pass(acc_cls, c, i, cls_words[c][:, i, :], cls_planes[4 * i : P, c, :])
         logit = keep.tile([BATCH, PROPOSALS], F32)
-        nc.vector.tensor_tensor(out=logit[:], in0=acc_cls[:, PROPOSALS:], in1=bias_diff[:], op=ALU.add)
-        nc.vector.tensor_tensor(out=logit[:], in0=logit[:], in1=acc_cls[:, 0:PROPOSALS], op=ALU.subtract)
-        nc.scalar.activation(out=logit[:], in_=logit[:], func=ACT.Tanh, scale=0.5)
-        nc.vector.tensor_scalar(
-            out=results[:, 4, :], in0=logit[:], scalar1=0.5, scalar2=0.5, op0=ALU.mult, op1=ALU.add
-        )
-        out_sb = keep.tile([BATCH, PROPOSALS, 5], F32)
-        cut = 168
-        nc.scalar.copy(out=out_sb[:, cut:, :], in_=results[:, :, cut:].rearrange("b f n -> b n f"))
-        nc.vector.tensor_copy(out=out_sb[:, 0:cut, :], in_=results[:, :, 0:cut].rearrange("b f n -> b n f"))
-        nc.sync.dma_start(out=out[:, 0:cut, :], in_=out_sb[:, 0:cut, :])
-        nc.sync.dma_start(out=out[:, cut:, :], in_=out_sb[:, cut:, :])
+        halves = [slice(first, first + HALF) for first in range(0, PROPOSALS, HALF)]
+        for n in halves:
+            c1 = slice(PROPOSALS + n.start, PROPOSALS + n.stop)
+            nc.vector.tensor_tensor(out=logit[:, n], in0=acc_cls[:, c1], in1=bias_diff[:, n], op=ALU.add)
+        for n in halves:
+            nc.vector.tensor_tensor(out=logit[:, n], in0=logit[:, n], in1=acc_cls[:, n], op=ALU.subtract)
+            nc.scalar.activation(out=logit[:, n], in_=logit[:, n], func=ACT.Tanh, scale=0.5)
+        for n in halves:
+            nc.vector.tensor_scalar(
+                out=out_sb[:, n, 4], in0=logit[:, n], scalar1=0.5, scalar2=0.5, op0=ALU.mult, op1=ALU.add
+            )
+            nc.sync.dma_start(out=out[:, n, :], in_=out_sb[:, n, :])

@@ -28,6 +28,7 @@ CHUNKS = GROUPS // CHUNK
 QUADS = 4
 BOX_LAG = 5
 BOX_BUFS = 6
+CLS_EARLY = 2
 assert CHUNKS - 1 - BOX_BUFS + BOX_LAG < CHUNKS - 1
 HALF = PROPOSALS // 2
 STRIDE = 16.0
@@ -143,6 +144,8 @@ def tile_classifiermodel_k_kernel(
             load_conv(c)
         for c in range(BOX_BUFS):
             load_box(c)
+        for c in range(CLS_EARLY):
+            load_cls(c)
 
         ident_f32 = keep.tile([P, P], F32)
         nc.vector.tensor_copy(out=ident_f32[:], in_=ident_bf[:])
@@ -270,7 +273,7 @@ def tile_classifiermodel_k_kernel(
             if c >= 0:
                 after_box(c)
             if s == CHUNKS - 1:
-                for later in range(CHUNKS):
+                for later in range(CLS_EARLY, CHUNKS):
                     load_cls(later)
             if s >= 1:
                 quantise_hidden(s - 1)

@@ -30,6 +30,8 @@ BOX_LAG = 5
 BOX_BUFS = 6
 CLS_EARLY = 2
 assert CHUNKS - 1 - BOX_BUFS + BOX_LAG < CHUNKS - 1
+LOGIT_0 = slice(0, PROPOSALS)
+LOGIT_1 = slice(PROPOSALS, CLS_COLS)
 HALF = PROPOSALS // 2
 STRIDE = 16.0
 CLIP = 10.0
@@ -97,10 +99,14 @@ def tile_classifiermodel_k_kernel(
             cls_words[c] = wide_pool.tile([P, CHUNK, CLS_COLS], U32, name="cls_words", tag="wide", align_bytes=64)
             groups_a_load = 1 if c == CHUNKS - 1 else 2
             for i in range(0, CHUNK, groups_a_load):
-                nc.sync.dma_start(
-                    out=cls_words[c][:, i : i + groups_a_load, :].bitcast(I32),
-                    in_=cls_w_words[first + i : first + i + groups_a_load].rearrange("g p n t -> p g (n t)").bitcast(I32),
-                )
+                last_group = first + i == GROUPS - 1
+                for cols in (LOGIT_1, LOGIT_0) if last_group else (slice(0, CLS_COLS),):
+                    nc.sync.dma_start(
+                        out=cls_words[c][:, i : i + groups_a_load, cols].bitcast(I32),
+                        in_=cls_w_words[first + i : first + i + groups_a_load, :, cols, :]
+                        .rearrange("g p n t -> p g (n t)")
+                        .bitcast(I32),
+                    )
 
         load_conv(0)
         ident_bf = keep.tile([P, P], BF16)
@@ -196,7 +202,6 @@ def tile_classifiermodel_k_kernel(
             nc.vector.tensor_tensor(out=x_early[:], in0=r[:, 0, :], in1=x_early[:], op=ALU.subtract)
             nc.vector.tensor_tensor(out=bias_diff[:], in0=bias_c1, in1=bias_c0, op=ALU.subtract)
 
-        acc_cls = acc_pool.tile([BATCH, CLS_COLS], F32)
         acc_b23 = acc_pool.tile([BATCH, 2 * PROPOSALS], F32)
         acc_b1 = acc_pool.tile([BATCH, PROPOSALS], F32)
         sorted_sums = {}
@@ -299,16 +304,17 @@ def tile_classifiermodel_k_kernel(
         out_sb = keep.tile([BATCH, PROPOSALS, 5], F32)
         nc.vector.tensor_copy(out=out_sb[:, :, 0:4], in_=results[:].rearrange("b f n -> b n f"))
 
+        acc_c1 = sums_pool.tile([BATCH, PROPOSALS], F32, name="acc_c1", tag="sums")
+        acc_c0 = sums_pool.tile([BATCH, PROPOSALS], F32, name="acc_c0", tag="sums")
         for c in range(CHUNKS):
             for i in range(CHUNK):
-                head_pass(acc_cls, c, i, cls_words[c][:, i, :], cls_planes[4 * i : P, c, :])
+                head_pass(acc_c1, c, i, cls_words[c][:, i, LOGIT_1], cls_planes[4 * i : P, c, LOGIT_1])
+                head_pass(acc_c0, c, i, cls_words[c][:, i, LOGIT_0], cls_planes[4 * i : P, c, LOGIT_0])
         logit = keep.tile([BATCH, PROPOSALS], F32)
         halves = [slice(first, first + HALF) for first in range(0, PROPOSALS, HALF)]
+        nc.vector.tensor_tensor(out=logit[:], in0=acc_c1[:], in1=bias_diff[:], op=ALU.add)
         for n in halves:
-            c1 = slice(PROPOSALS + n.start, PROPOSALS + n.stop)
-            nc.vector.tensor_tensor(out=logit[:, n], in0=acc_cls[:, c1], in1=bias_diff[:, n], op=ALU.add)
-        for n in halves:
-            nc.vector.tensor_tensor(out=logit[:, n], in0=logit[:, n], in1=acc_cls[:, n], op=ALU.subtract)
+            nc.vector.tensor_tensor(out=logit[:, n], in0=logit[:, n], in1=acc_c0[:, n], op=ALU.subtract)
             nc.scalar.activation(out=logit[:, n], in_=logit[:, n], func=ACT.Tanh, scale=0.5)
         for n in halves:
             nc.vector.tensor_scalar(

@@ -127,16 +127,13 @@ def tile_classifiermodel_k_kernel(
         nc.vector.memset(box_planes[:].bitcast(I32), 0)
         nc.vector.memset(cls_planes[:].bitcast(I32), 0)
         nc.scalar.dma_start(out=conv_b_rows[0:GROUPS, :], in_=conv_b.rearrange("(g k) -> g k", k=K_PASS))
-        nc.scalar.dma_start(out=bias_row[0:1, 0:CLS_COLS], in_=cls_b.unsqueeze(0))
-        nc.scalar.dma_start(out=bias_row[0:1, CLS_COLS:], in_=bbox_b[BOX_SKIP:].unsqueeze(0))
         roi_sb = keep.tile([BATCH, PROPOSALS * 4], BF16)
-        nc.scalar.dma_start(out=roi_sb[:], in_=roi.rearrange("b n f -> b (n f)"))
         nc.scalar.activation(out=table[:], in_=table[:], func=ACT.Exp)
 
         for quad in range(QUADS):
-            nc.gpsimd.dma_start(
-                out=conv_planes[32 * quad : 32 * quad + 16, :].bitcast(F32),
-                in_=conv_w_scales[0, 4 * quad : 4 * quad + 4, :].rearrange("r (i n) -> i r n", i=CHUNK).bitcast(F32),
+            nc.sync.dma_start(
+                out=conv_planes[32 * quad : 32 * quad + 16, :].bitcast(I32),
+                in_=conv_w_scales[0, 4 * quad : 4 * quad + 4, :].rearrange("r (i n) -> i r n", i=CHUNK).bitcast(I32),
             )
         for planes, scales in ((box_planes, bbox_w_scales[:, :, BOX_SKIP:]), (cls_planes, cls_w_scales)):
             for quad in range(QUADS):
@@ -150,6 +147,9 @@ def tile_classifiermodel_k_kernel(
             load_conv(c)
         for c in range(BOX_BUFS):
             load_box(c)
+        nc.sync.dma_start(out=bias_row[0:1, 0:CLS_COLS], in_=cls_b.unsqueeze(0))
+        nc.sync.dma_start(out=bias_row[0:1, CLS_COLS:], in_=bbox_b[BOX_SKIP:].unsqueeze(0))
+        nc.sync.dma_start(out=roi_sb[:], in_=roi.rearrange("b n f -> b (n f)"))
         for c in range(CLS_EARLY):
             load_cls(c)
 

@@ -86,10 +86,10 @@ def tile_classifiermodel_k_kernel(
         def load_box(c):
             first = c * CHUNK
             box_words[c] = box_pool.tile([P, CHUNK, BOX_COLS], U32, name="box_words", align_bytes=64)
-            for i in range(0, CHUNK, 2):
+            for i in range(CHUNK):
                 nc.sync.dma_start(
-                    out=box_words[c][:, i : i + 2, :].bitcast(I32),
-                    in_=bbox_w_words[first + i : first + i + 2, :, BOX_SKIP:, :]
+                    out=box_words[c][:, i : i + 1, :].bitcast(I32),
+                    in_=bbox_w_words[first + i : first + i + 1, :, BOX_SKIP:, :]
                     .rearrange("g p n t -> p g (n t)")
                     .bitcast(I32),
                 )
@@ -97,7 +97,7 @@ def tile_classifiermodel_k_kernel(
         def load_cls(c):
             first = c * CHUNK
             cls_words[c] = wide_pool.tile([P, CHUNK, CLS_COLS], U32, name="cls_words", tag="wide", align_bytes=64)
-            groups_a_load = 1 if c == CHUNKS - 1 else 2
+            groups_a_load = 1
             for i in range(0, CHUNK, groups_a_load):
                 last_group = first + i == GROUPS - 1
                 for cols in (LOGIT_1, LOGIT_0) if last_group else (slice(0, CLS_COLS),):

@@ -63,7 +63,7 @@ def tile_classifiermodel_k_kernel(
     with ExitStack() as stack:
         stack.enter_context(tc.manual_schedule())
         keep = stack.enter_context(tc.tile_pool(name="keep", bufs=1))
-        wide_pool = stack.enter_context(tc.tile_pool(name="wide", bufs=CHUNKS))
+        wide_pool = stack.enter_context(tc.tile_pool(name="wide", bufs=1))
         box_pool = stack.enter_context(tc.tile_pool(name="box", bufs=BOX_BUFS))
         work = stack.enter_context(tc.tile_pool(name="work", bufs=2))
         flat_pool = stack.enter_context(tc.tile_pool(name="flat", bufs=CHUNKS))
@@ -71,15 +71,14 @@ def tile_classifiermodel_k_kernel(
         turn_pool = stack.enter_context(tc.psum_pool(name="turn", bufs=3))
         sums_pool = stack.enter_context(tc.psum_pool(name="sums", bufs=2))
 
-        conv_words = {}
-        cls_words = {}
+        conv_words = wide_pool.tile([P, HIDDEN], U32, name="conv_words", tag="wide", align_bytes=64)
+        cls_words = wide_pool.tile([P, GROUPS, CLS_COLS], U32, name="cls_words", tag="wide", align_bytes=64)
         box_words = {}
 
-        def load_conv(c):
-            conv_words[c] = wide_pool.tile([P, CHUNK * K_PASS], U32, name="conv_words", tag="wide", align_bytes=64)
-            cols = slice(c * CHUNK * K_PASS, (c + 1) * CHUNK * K_PASS)
+        def load_conv(c, chunks):
+            cols = slice(c * CHUNK * K_PASS, (c + chunks) * CHUNK * K_PASS)
             nc.sync.dma_start(
-                out=conv_words[c][:].bitcast(I32),
+                out=conv_words[:, cols].bitcast(I32),
                 in_=conv_w_words[0, :, cols, :].rearrange("p n t -> p (n t)").bitcast(I32),
             )
 
@@ -95,20 +94,14 @@ def tile_classifiermodel_k_kernel(
                 )
 
         def load_cls(c):
-            first = c * CHUNK
-            cls_words[c] = wide_pool.tile([P, CHUNK, CLS_COLS], U32, name="cls_words", tag="wide", align_bytes=64)
-            groups_a_load = 1
-            for i in range(0, CHUNK, groups_a_load):
-                last_group = first + i == GROUPS - 1
-                for cols in (LOGIT_1, LOGIT_0) if last_group else (slice(0, CLS_COLS),):
+            for g in range(c * CHUNK, (c + 1) * CHUNK):
+                for cols in (LOGIT_1, LOGIT_0) if g == GROUPS - 1 else (slice(0, CLS_COLS),):
                     nc.sync.dma_start(
-                        out=cls_words[c][:, i : i + groups_a_load, cols].bitcast(I32),
-                        in_=cls_w_words[first + i : first + i + groups_a_load, :, cols, :]
-                        .rearrange("g p n t -> p g (n t)")
-                        .bitcast(I32),
+                        out=cls_words[:, g : g + 1, cols].bitcast(I32),
+                        in_=cls_w_words[g : g + 1, :, cols, :].rearrange("g p n t -> p g (n t)").bitcast(I32),
                     )
 
-        load_conv(0)
+        load_conv(0, 1)
         ident_bf = keep.tile([P, P], BF16)
         make_identity(nc, ident_bf[:])
         feat_sb = keep.tile([BATCH, CHANNELS], BF16)
@@ -143,8 +136,9 @@ def tile_classifiermodel_k_kernel(
                         in_=scales[:, 4 * quad + r, :].rearrange("(c i) n -> i c n", i=CHUNK).bitcast(F32),
                     )
 
-        for c in range(1, CHUNKS):
-            load_conv(c)
+        load_conv(1, 1)
+        load_conv(2, 2)
+        load_conv(4, 4)
         for c in range(BOX_BUFS):
             load_box(c)
         nc.sync.dma_start(out=bias_row[0:1, 0:CLS_COLS], in_=cls_b.unsqueeze(0))
@@ -217,7 +211,7 @@ def tile_classifiermodel_k_kernel(
                 out=sums[:],
                 lhsT=feat_words[:].bitcast(FP8X4),
                 lhsT_scale=feat_plane[:],
-                rhs=conv_words[c][:, i * K_PASS : (i + 1) * K_PASS].bitcast(FP8X4),
+                rhs=conv_words[:, g * K_PASS : (g + 1) * K_PASS].bitcast(FP8X4),
                 rhs_scale=conv_planes[4 * plane : P, first : first + K_PASS],
                 start=True,
                 stop=True,
@@ -308,8 +302,8 @@ def tile_classifiermodel_k_kernel(
         acc_c0 = sums_pool.tile([BATCH, PROPOSALS], F32, name="acc_c0", tag="sums")
         for c in range(CHUNKS):
             for i in range(CHUNK):
-                head_pass(acc_c1, c, i, cls_words[c][:, i, LOGIT_1], cls_planes[4 * i : P, c, LOGIT_1])
-                head_pass(acc_c0, c, i, cls_words[c][:, i, LOGIT_0], cls_planes[4 * i : P, c, LOGIT_0])
+                head_pass(acc_c1, c, i, cls_words[:, c * CHUNK + i, LOGIT_1], cls_planes[4 * i : P, c, LOGIT_1])
+                head_pass(acc_c0, c, i, cls_words[:, c * CHUNK + i, LOGIT_0], cls_planes[4 * i : P, c, LOGIT_0])
         logit = keep.tile([BATCH, PROPOSALS], F32)
         halves = [slice(first, first + HALF) for first in range(0, PROPOSALS, HALF)]
         nc.vector.tensor_tensor(out=logit[:], in0=acc_c1[:], in1=bias_diff[:], op=ALU.add)

from contextlib import ExitStack

import concourse.mybir as mybir
from concourse.masks import make_identity

F32 = mybir.dt.float32
BF16 = mybir.dt.bfloat16
I32 = mybir.dt.int32
U32 = mybir.dt.uint32
U8 = mybir.dt.uint8
FP8X4 = mybir.dt.float8_e4m3fn_x4
ALU = mybir.AluOpType
ACT = mybir.ActivationFunctionType

P = 128
PACK = 4
K_PASS = P * PACK
BATCH = 128
CHANNELS = 512
HIDDEN = 16384
PROPOSALS = 256
CLS_COLS = 2 * PROPOSALS
BOX_SKIP = PROPOSALS
BOX_COLS = 3 * PROPOSALS
GROUPS = HIDDEN // K_PASS
CHUNK = 4
CHUNKS = GROUPS // CHUNK
QUADS = 4
BOX_LAG = 5
BOX_BUFS = 6
CLS_EARLY = 2
assert CHUNKS - 1 - BOX_BUFS + BOX_LAG < CHUNKS - 1
LOGIT_0 = slice(0, PROPOSALS)
LOGIT_1 = slice(PROPOSALS, CLS_COLS)
HALF = PROPOSALS // 2
STRIDE = 16.0
CLIP = 10.0

FLOPS = 2 * BATCH * CHANNELS * HIDDEN + 2 * BATCH * HIDDEN * (CLS_COLS + BOX_COLS)
BYTES = (
    (CHANNELS * HIDDEN + HIDDEN * (CLS_COLS + BOX_COLS)) * 33 // 32
    + 2 * (BATCH * CHANNELS + BATCH * PROPOSALS * 4 + HIDDEN + CLS_COLS + BOX_COLS)
    + 4 * BATCH * PROPOSALS * 5
)


def tile_classifiermodel_k_kernel(
    tc,
    features,
    roi,
    conv_w_words,
    conv_w_scales,
    conv_b,
    cls_w_words,
    cls_w_scales,
    cls_b,
    bbox_w_words,
    bbox_w_scales,
    bbox_b,
    out,
):
    nc = tc.nc
    with ExitStack() as stack:
        stack.enter_context(tc.manual_schedule())
        keep = stack.enter_context(tc.tile_pool(name="keep", bufs=1))
        wide_pool = stack.enter_context(tc.tile_pool(name="wide", bufs=1))
        box_pool = stack.enter_context(tc.tile_pool(name="box", bufs=BOX_BUFS))
        work = stack.enter_context(tc.tile_pool(name="work", bufs=2))
        flat_pool = stack.enter_context(tc.tile_pool(name="flat", bufs=CHUNKS))
        acc_pool = stack.enter_context(tc.psum_pool(name="acc", bufs=1))
        turn_pool = stack.enter_context(tc.psum_pool(name="turn", bufs=3))
        sums_pool = stack.enter_context(tc.psum_pool(name="sums", bufs=2))

        conv_words = wide_pool.tile([P, HIDDEN], U32, name="conv_words", tag="wide", align_bytes=64)
        cls_words = wide_pool.tile([P, GROUPS, CLS_COLS], U32, name="cls_words", tag="wide", align_bytes=64)
        box_words = {}

        def load_conv(c, chunks):
            cols = slice(c * CHUNK * K_PASS, (c + chunks) * CHUNK * K_PASS)
            nc.sync.dma_start(
                out=conv_words[:, cols].bitcast(I32),
                in_=conv_w_words[0, :, cols, :].rearrange("p n t -> p (n t)").bitcast(I32),
            )

        def load_box(c):
            first = c * CHUNK
            box_words[c] = box_pool.tile([P, CHUNK, BOX_COLS], U32, name="box_words", align_bytes=64)
            for i in range(CHUNK):
                nc.sync.dma_start(
                    out=box_words[c][:, i : i + 1, :].bitcast(I32),
                    in_=bbox_w_words[first + i : first + i + 1, :, BOX_SKIP:, :]
                    .rearrange("g p n t -> p g (n t)")
                    .bitcast(I32),
                )

        def load_cls(c):
            for g in range(c * CHUNK, (c + 1) * CHUNK):
                for cols in (LOGIT_1, LOGIT_0) if g == GROUPS - 1 else (slice(0, CLS_COLS),):
                    nc.sync.dma_start(
                        out=cls_words[:, g : g + 1, cols].bitcast(I32),
                        in_=cls_w_words[g : g + 1, :, cols, :].rearrange("g p n t -> p g (n t)").bitcast(I32),
                    )

        load_conv(0, 1)
        ident_bf = keep.tile([P, P], BF16)
        make_identity(nc, ident_bf[:])
        feat_sb = keep.tile([BATCH, CHANNELS], BF16)
        nc.scalar.dma_start(out=feat_sb[:], in_=features.rearrange("b h w c -> b (h w c)"))

        conv_planes = keep.tile([P, HIDDEN // CHUNK], U8, align_bytes=64)
        cls_planes = keep.tile([P, CHUNKS, CLS_COLS], U8, align_bytes=64)
        box_planes = keep.tile([P, CHUNKS, BOX_COLS], U8, align_bytes=64)
        conv_b_rows = keep.tile([P, K_PASS], BF16)
        bias_row = keep.tile([P, CLS_COLS + BOX_COLS], BF16)
        table = keep.tile([P, 1], F32)
        nc.vector.memset(conv_planes[:].bitcast(I32), 0)
        nc.vector.memset(conv_b_rows[:], 0.0)
        nc.vector.memset(bias_row[:], 0.0)
        nc.vector.memset(table[:], 0.0)
        nc.vector.memset(box_planes[:].bitcast(I32), 0)
        nc.vector.memset(cls_planes[:].bitcast(I32), 0)
        nc.scalar.dma_start(out=conv_b_rows[0:GROUPS, :], in_=conv_b.rearrange("(g k) -> g k", k=K_PASS))
        roi_sb = keep.tile([BATCH, PROPOSALS * 4], BF16)
        nc.scalar.activation(out=table[:], in_=table[:], func=ACT.Exp)

        for quad in range(QUADS):
            nc.sync.dma_start(
                out=conv_planes[32 * quad : 32 * quad + 16, :].bitcast(I32),
                in_=conv_w_scales[0, 4 * quad : 4 * quad + 4, :].rearrange("r (i n) -> i r n", i=CHUNK).bitcast(I32),
            )
        for planes, scales in ((box_planes, bbox_w_scales[:, :, BOX_SKIP:]), (cls_planes, cls_w_scales)):
            for quad in range(QUADS):
                for r in range(4):
                    nc.gpsimd.dma_start(
                        out=planes[32 * quad + r : 32 * quad + 16 : 4, :, :].bitcast(F32),
                        in_=scales[:, 4 * quad + r, :].rearrange("(c i) n -> i c n", i=CHUNK).bitcast(F32),
                    )

        load_conv(1, 1)
        load_conv(2, 2)
        load_conv(4, 4)
        for c in range(BOX_BUFS):
            load_box(c)
        nc.sync.dma_start(out=bias_row[0:1, 0:CLS_COLS], in_=cls_b.unsqueeze(0))
        nc.sync.dma_start(out=bias_row[0:1, CLS_COLS:], in_=bbox_b[BOX_SKIP:].unsqueeze(0))
        nc.sync.dma_start(out=roi_sb[:], in_=roi.rearrange("b n f -> b (n f)"))
        for c in range(CLS_EARLY):
            load_cls(c)

        ident_f32 = keep.tile([P, P], F32)
        nc.vector.tensor_copy(out=ident_f32[:], in_=ident_bf[:])
        ones = keep.tile([P, P], BF16)
        nc.vector.memset(ones[:], 1.0)

        def k_onto_partitions(rows_sb):
            turned = turn_pool.tile([P, PACK, P], BF16, name="turned_bf", tag="turned")
            for t in range(PACK):
                nc.tensor.transpose(out=turned[:, t, :], in_=rows_sb[:, t:K_PASS:PACK], identity=ident_bf[:])
            return turned

        feat_turned = k_onto_partitions(feat_sb)
        feat_grouped = keep.tile([P, BATCH, PACK], BF16, align_bytes=64)
        nc.vector.tensor_copy(out=feat_grouped[:], in_=feat_turned[:].rearrange("p t b -> p b t"))
        feat_words = keep.tile([P, BATCH], U32, align_bytes=64)
        feat_plane = keep.tile([P, BATCH], U8, align_bytes=64)
        nc.vector.quantize_mx(
            out=feat_words[:].bitcast(FP8X4),
            scales=feat_plane[:],
            in_=feat_grouped[:].rearrange("p b t -> p (b t)"),
        )

        conv_b_turned = k_onto_partitions(conv_b_rows)
        conv_bias = keep.tile([P, GROUPS, PACK], F32)
        nc.vector.tensor_copy(out=conv_bias[:], in_=conv_b_turned[:, :, 0:GROUPS].rearrange("p t g -> p g t"))

        head_bias = keep.tile([BATCH, CLS_COLS + BOX_COLS], F32)
        bias_c0 = head_bias[:, 0:PROPOSALS]
        bias_c1 = head_bias[:, PROPOSALS:CLS_COLS]
        bias_b1 = head_bias[:, CLS_COLS : CLS_COLS + PROPOSALS]
        bias_b23 = head_bias[:, CLS_COLS + PROPOSALS :]
        r = keep.tile([BATCH, 4, PROPOSALS], F32)
        results = keep.tile([BATCH, 4, PROPOSALS], F32)
        x_early = keep.tile([BATCH, PROPOSALS], F32)
        bias_diff = keep.tile([BATCH, PROPOSALS], F32)

        def prepare_end():
            for first in range(0, CLS_COLS + BOX_COLS, 512):
                width = min(512, CLS_COLS + BOX_COLS - first)
                cols = slice(first, first + width)
                spread = turn_pool.tile([P, 512], F32, name="spread", tag="turned")
                nc.tensor.matmul(out=spread[:, 0:width], lhsT=ones[:], rhs=bias_row[:, cols], start=True, stop=True)
                nc.scalar.copy(out=head_bias[:, cols], in_=spread[:, 0:width])
            nc.vector.tensor_scalar_mul(out=r[:], in0=roi_sb[:].rearrange("b (n f) -> b f n", f=4), scalar1=STRIDE)
            nc.vector.tensor_copy(out=results[:, 1, :], in_=r[:, 1, :])
            nc.vector.tensor_tensor(out=x_early[:], in0=bias_b1, in1=r[:, 3, :], op=ALU.mult)
            nc.vector.tensor_tensor(out=x_early[:], in0=r[:, 0, :], in1=x_early[:], op=ALU.subtract)
            nc.vector.tensor_tensor(out=bias_diff[:], in0=bias_c1, in1=bias_c0, op=ALU.subtract)

        acc_b23 = acc_pool.tile([BATCH, 2 * PROPOSALS], F32)
        acc_b1 = acc_pool.tile([BATCH, PROPOSALS], F32)
        sorted_sums = {}
        flat_words = {}
        flat_planes = {}

        def conv_pass(c, i):
            g = c * CHUNK + i
            plane = g // (GROUPS // CHUNK)
            first = (g % (GROUPS // CHUNK)) * K_PASS
            sums = sums_pool.tile([BATCH, K_PASS], F32)
            nc.tensor.matmul_mx(
                out=sums[:],
                lhsT=feat_words[:].bitcast(FP8X4),
                lhsT_scale=feat_plane[:],
                rhs=conv_words[:, g * K_PASS : (g + 1) * K_PASS].bitcast(FP8X4),
                rhs_scale=conv_planes[4 * plane : P, first : first + K_PASS],
                start=True,
                stop=True,
            )
            nc.scalar.copy(out=sorted_sums[c][:, i, :, :], in_=sums[:].rearrange("b (p t) -> b t p", t=PACK))

        def quantise_hidden(c):
            hidden = work.tile([P, CHUNK, BATCH, PACK], BF16, align_bytes=64)
            for i in range(CHUNK):
                turned = turn_pool.tile([P, PACK, BATCH], F32)
                for t in range(PACK):
                    nc.tensor.transpose(out=turned[:, t, :], in_=sorted_sums[c][:, i, t, :], identity=ident_f32[:])
                nc.vector.tensor_tensor(
                    out=hidden[:, i, :, :],
                    in0=turned[:].rearrange("p t b -> p b t"),
                    in1=conv_bias[:, c * CHUNK + i, :].unsqueeze(1).to_broadcast([P, BATCH, PACK]),
                    op=ALU.add,
                )
            hidden_flat = hidden[:].rearrange("p i b t -> p (i b t)")
            nc.vector.tensor_scalar_max(out=hidden_flat, in0=hidden_flat, scalar1=0.0)
            flat_words[c] = flat_pool.tile([P, CHUNK, BATCH], U32, name="flat_words", align_bytes=64)
            flat_planes[c] = flat_pool.tile([P, CHUNK, BATCH], U8, name="flat_planes", align_bytes=64)
            nc.vector.quantize_mx(
                out=flat_words[c][:].rearrange("p i b -> p (i b)").bitcast(FP8X4),
                scales=flat_planes[c][:].rearrange("p i b -> p (i b)"),
                in_=hidden_flat,
            )

        def head_pass(acc, c, i, words, plane):
            g = c * CHUNK + i
            nc.tensor.matmul_mx(
                out=acc[:],
                lhsT=flat_words[c][:, i, :].bitcast(FP8X4),
                lhsT_scale=flat_planes[c][:, i, :],
                rhs=words.bitcast(FP8X4),
                rhs_scale=plane,
                start=(g == 0),
                stop=(g == GROUPS - 1),
            )

        def box_passes(c, i):
            head_pass(acc_b23, c, i, box_words[c][:, i, PROPOSALS:], box_planes[4 * i : P, c, PROPOSALS:])
            head_pass(acc_b1, c, i, box_words[c][:, i, 0:PROPOSALS], box_planes[4 * i : P, c, 0:PROPOSALS])

        def after_box(c):
            if c + BOX_BUFS < CHUNKS:
                load_box(c + BOX_BUFS)

        for s in range(CHUNKS + 1):
            c = s - BOX_LAG
            if s < CHUNKS:
                sorted_sums[s] = work.tile([BATCH, CHUNK, PACK, P], F32, name="sorted_sums")
            for i in range(CHUNK):
                if s < CHUNKS:
                    conv_pass(s, i)
                if c >= 0:
                    box_passes(c, i)
            if c >= 0:
                after_box(c)
            if s == CHUNKS - 1:
                for later in range(CLS_EARLY, CHUNKS):
                    load_cls(later)
            if s >= 1:
                quantise_hidden(s - 1)
        prepare_end()
        for c in range(CHUNKS + 1 - BOX_LAG, CHUNKS):
            for i in range(CHUNK):
                box_passes(c, i)
            after_box(c)

        growth = keep.tile([BATCH, 2 * PROPOSALS], F32)
        nc.vector.tensor_tensor(out=growth[:], in0=acc_b23[:], in1=bias_b23, op=ALU.add)
        nc.vector.tensor_scalar(out=growth[:], in0=growth[:], scalar1=CLIP, scalar2=-CLIP, op0=ALU.min, op1=ALU.max)
        nc.scalar.activation(out=growth[:], in_=growth[:], func=ACT.Exp)
        shift = keep.tile([BATCH, PROPOSALS], F32)
        nc.vector.tensor_tensor(out=shift[:], in0=acc_b1[:], in1=r[:, 3, :], op=ALU.mult)
        nc.vector.tensor_tensor(out=results[:, 0, :], in0=x_early[:], in1=shift[:], op=ALU.subtract)
        nc.vector.tensor_tensor(
            out=results[:, 2:4, :].rearrange("b f n -> b (f n)"),
            in0=r[:, 2:4, :].rearrange("b f n -> b (f n)"),
            in1=growth[:],
            op=ALU.mult,
        )
        out_sb = keep.tile([BATCH, PROPOSALS, 5], F32)
        nc.vector.tensor_copy(out=out_sb[:, :, 0:4], in_=results[:].rearrange("b f n -> b n f"))

        acc_c1 = sums_pool.tile([BATCH, PROPOSALS], F32, name="acc_c1", tag="sums")
        acc_c0 = sums_pool.tile([BATCH, PROPOSALS], F32, name="acc_c0", tag="sums")
        for c in range(CHUNKS):
            for i in range(CHUNK):
                head_pass(acc_c1, c, i, cls_words[:, c * CHUNK + i, LOGIT_1], cls_planes[4 * i : P, c, LOGIT_1])
                head_pass(acc_c0, c, i, cls_words[:, c * CHUNK + i, LOGIT_0], cls_planes[4 * i : P, c, LOGIT_0])
        logit = keep.tile([BATCH, PROPOSALS], F32)
        halves = [slice(first, first + HALF) for first in range(0, PROPOSALS, HALF)]
        nc.vector.tensor_tensor(out=logit[:], in0=acc_c1[:], in1=bias_diff[:], op=ALU.add)
        for n in halves:
            nc.vector.tensor_tensor(out=logit[:, n], in0=logit[:, n], in1=acc_c0[:, n], op=ALU.subtract)
            nc.scalar.activation(out=logit[:, n], in_=logit[:, n], func=ACT.Tanh, scale=0.5)
        for n in halves:
            nc.vector.tensor_scalar(
                out=out_sb[:, n, 4], in0=logit[:, n], scalar1=0.5, scalar2=0.5, op0=ALU.mult, op1=ALU.add
            )
            nc.sync.dma_start(out=out[:, n, :], in_=out_sb[:, n, :])
